import numpy as np
import ml_dtypes


def mxq(x, axis, fmt="e4m3"):
    dtype, down = {"e4m3": (ml_dtypes.float8_e4m3fn, 7), "e5m2": (ml_dtypes.float8_e5m2, 14)}[fmt]
    v = np.moveaxis(np.asarray(x, np.float32).astype(ml_dtypes.bfloat16).astype(np.float64), axis, -1)
    blocks = v.reshape(v.shape[:-1] + (-1, 32))
    amax = np.abs(blocks).max(-1, keepdims=True)
    byte = np.maximum(np.where(amax > 0, np.frexp(amax)[1] - 1 + 127, 0) - down, 1)
    scale = np.exp2(byte - 127.0)
    codes = (blocks / scale).astype(np.float32).astype(dtype).astype(np.float64)
    return np.moveaxis((codes * scale).reshape(v.shape), -1, axis)


WIDE = False


def mx_kscale(k):
    if not WIDE:
        return np.ones(k)
    levels = np.array([20, -20, 10, -10, 0])
    a = np.random.permutation(np.resize(levels, k // 512 * 4)).reshape(k // 512, 4)
    idx = np.arange(k)
    return np.exp2(a[idx // 512, idx % 128 // 32])


BF16 = ml_dtypes.bfloat16


def bf(x):
    return np.asarray(x, np.float32).astype(BF16)


def f64(x):
    return np.asarray(x).astype(np.float64)


B, S, IN, OUT = 2, 256, 4096, 1024
T = B * S


def setup_inputs():
    s = mx_kscale(T).reshape(B, S, 1)
    x = np.random.standard_normal((B, S, IN)) * s
    w = np.random.standard_normal((OUT, IN)) * (IN ** -0.5)
    b = np.random.standard_normal(OUT) * 0.1
    g = np.random.standard_normal((B, S, OUT)) * np.exp2(np.random.randint(-12, 1, (B, S, 1))) / s
    return {"input_": bf(x), "weight": bf(w), "bias": bf(b), "grad_out": bf(g)}


def reference(input_, weight, bias, grad_out):
    x = f64(input_).reshape(T, IN)
    g = f64(grad_out).reshape(T, OUT)
    return mxq(g, 0, "e5m2").T @ mxq(x, 0, "e4m3")

@@ -1,0 +1,118 @@
+from contextlib import ExitStack
+
+import concourse.mybir as mybir
+
+BF16 = mybir.dt.bfloat16
+F32 = mybir.dt.float32
+U32 = mybir.dt.uint32
+U8 = mybir.dt.uint8
+E4M3X4 = mybir.dt.float8_e4m3fn_x4
+E5M2X4 = mybir.dt.float8_e5m2_x4
+
+P = 128
+PACK = 4
+TOKENS = 512
+IN = 4096
+OUT = 1024
+N_TILE = 512
+BLOCKS = OUT // P
+HEAD = 1536
+REST = IN - HEAD
+
+FLOPS = 2 * TOKENS * IN * OUT
+BYTES = TOKENS * IN * 2 + TOKENS * OUT * 2 + OUT * IN * 4
+
+
+def tile_terowparallellinear_kernel(tc, input_, weight, bias, grad_out, out):
+    nc = tc.nc
+    x = input_.flatten_outer_dims()
+    g = grad_out.flatten_outer_dims()
+
+    with ExitStack() as ctx:
+        keep = ctx.enter_context(tc.tile_pool(name="keep", bufs=1))
+        stage_a = ctx.enter_context(tc.tile_pool(name="stage_a", bufs=BLOCKS))
+        stage_b = ctx.enter_context(tc.tile_pool(name="stage_b", bufs=6))
+        psum = ctx.enter_context(tc.psum_pool(name="psum", bufs=8))
+        ctx.enter_context(tc.manual_schedule())
+
+        xh_raw = keep.tile([P, PACK, HEAD], BF16, name="xh_raw")
+        xr_raw = keep.tile([P, PACK, REST], BF16, name="xr_raw")
+        g_raw = keep.tile([P, PACK, OUT], BF16, name="g_raw")
+        x_grp = keep.tile([P, IN, PACK], BF16, name="x_grp", align_bytes=64)
+        g_grp = keep.tile([P, OUT, PACK], BF16, name="g_grp", align_bytes=64)
+        x_codes = keep.tile([P, IN], U32, name="x_codes", align_bytes=64)
+        x_scales = keep.tile([P, IN], U8, name="x_scales", align_bytes=64)
+        g_codes = keep.tile([P, OUT], U32, name="g_codes", align_bytes=64)
+        g_scales = keep.tile([P, OUT], U8, name="g_scales", align_bytes=64)
+
+        nc.sync.dma_start(out=xh_raw[:], in_=x[:, 0:HEAD].rearrange("(p j) w -> p j w", j=PACK))
+        nc.sync.dma_start(out=g_raw[:], in_=g.rearrange("(p j) w -> p j w", j=PACK))
+        nc.sync.dma_start(out=xr_raw[:], in_=x[:, HEAD:IN].rearrange("(p j) w -> p j w", j=PACK))
+
+        def regroup(copy, grp, raw, base, lo, hi):
+            copy(
+                out=grp[:, lo:hi, :].rearrange("p (c i) t -> p c t i", i=4),
+                in_=raw[:, :, lo - base : hi - base].rearrange("p t (c i) -> p c t i", i=4),
+            )
+
+        def quantise(grp, codes, scales, fmt, lo, hi):
+            nc.vector.quantize_mx(
+                out=codes[:, lo:hi].bitcast(fmt),
+                scales=scales[:, lo:hi],
+                in_=grp[:, lo:hi, :].rearrange("p w j -> p (w j)"),
+            )
+
+        def quantise_x(lo, hi):
+            quantise(x_grp, x_codes, x_scales, E4M3X4, lo, hi)
+
+        def quantise_g(lo, hi):
+            quantise(g_grp, g_codes, g_scales, E5M2X4, lo, hi)
+
+        def product(b, n, copy, dest):
+            acc = psum.tile([P, N_TILE], F32, name="acc")
+            nc.tensor.matmul_mx(
+                out=acc[:],
+                lhsT=g_codes[:, b * P : (b + 1) * P].bitcast(E5M2X4),
+                lhsT_scale=g_scales[:, b * P : (b + 1) * P],
+                rhs=x_codes[:, n * N_TILE : (n + 1) * N_TILE].bitcast(E4M3X4),
+                rhs_scale=x_scales[:, n * N_TILE : (n + 1) * N_TILE],
+                start=True,
+                stop=True,
+            )
+            copy(out=dest, in_=acc[:])
+
+        vcopy = nc.vector.tensor_copy
+        scopy = nc.scalar.copy
+
+        regroup(vcopy, x_grp, xh_raw, 0, 0, 768)
+        regroup(scopy, x_grp, xh_raw, 0, 768, 1536)
+        quantise_x(0, 512)
+        regroup(vcopy, g_grp, g_raw, 0, 0, 512)
+        regroup(scopy, g_grp, g_raw, 0, 512, 1024)
+        quantise_x(512, 1024)
+        quantise_g(0, 512)
+        quantise_x(1024, 1536)
+        quantise_g(512, 1024)
+
+        head_tiles = HEAD // N_TILE
+        for b in range(BLOCKS):
+            res = stage_a.tile([P, HEAD], F32, name="res_a")
+            for n in range(head_tiles):
+                copy = vcopy if (b < 3 and n == head_tiles - 1) else scopy
+                product(b, n, copy, res[:, n * N_TILE : (n + 1) * N_TILE])
+            nc.sync.dma_start(out=out[b * P : (b + 1) * P, 0:HEAD], in_=res[:])
+            if b == 2:
+                regroup(vcopy, x_grp, xr_raw, HEAD, 1536, 2560)
+                regroup(vcopy, x_grp, xr_raw, HEAD, 2560, 3584)
+                quantise_x(1536, 2560)
+                regroup(vcopy, x_grp, xr_raw, HEAD, 3584, 4096)
+                quantise_x(2560, 3584)
+                quantise_x(3584, 4096)
+
+        rest_tiles = REST // N_TILE
+        for b in range(BLOCKS):
+            res = stage_b.tile([P, REST], F32, name="res_b")
+            for n in range(rest_tiles):
+                copy = scopy if (n + b) % 2 == 0 else vcopy
+                product(b, head_tiles + n, copy, res[:, n * N_TILE : (n + 1) * N_TILE])
+            nc.sync.dma_start(out=out[b * P : (b + 1) * P, HEAD:IN], in_=res[:])

@@ -16,8 +16,9 @@ IN = 4096
 OUT = 1024
 N_TILE = 512
 BLOCKS = OUT // P
-HEAD = 1536
-REST = IN - HEAD
+LOADS = (0, 1024, 2048, 4096)
+SPLIT_ROWS = 4
+EARLY_V = 3
 
 FLOPS = 2 * TOKENS * IN * OUT
 BYTES = TOKENS * IN * 2 + TOKENS * OUT * 2 + OUT * IN * 4
@@ -30,14 +31,17 @@ def tile_terowparallellinear_kernel(tc, input_, weight, bias, grad_out, out):
 
     with ExitStack() as ctx:
         keep = ctx.enter_context(tc.tile_pool(name="keep", bufs=1))
-        stage_a = ctx.enter_context(tc.tile_pool(name="stage_a", bufs=BLOCKS))
-        stage_b = ctx.enter_context(tc.tile_pool(name="stage_b", bufs=6))
+        stage2 = ctx.enter_context(tc.tile_pool(name="stage2", bufs=8))
+        stage4 = ctx.enter_context(tc.tile_pool(name="stage4", bufs=4))
+        stage6 = ctx.enter_context(tc.tile_pool(name="stage6", bufs=3))
         psum = ctx.enter_context(tc.psum_pool(name="psum", bufs=8))
         ctx.enter_context(tc.manual_schedule())
 
-        xh_raw = keep.tile([P, PACK, HEAD], BF16, name="xh_raw")
-        xr_raw = keep.tile([P, PACK, REST], BF16, name="xr_raw")
         g_raw = keep.tile([P, PACK, OUT], BF16, name="g_raw")
+        x_raw = [
+            keep.tile([P, PACK, LOADS[i + 1] - LOADS[i]], BF16, name="x_raw%d" % i)
+            for i in range(3)
+        ]
         x_grp = keep.tile([P, IN, PACK], BF16, name="x_grp", align_bytes=64)
         g_grp = keep.tile([P, OUT, PACK], BF16, name="g_grp", align_bytes=64)
         x_codes = keep.tile([P, IN], U32, name="x_codes", align_bytes=64)
@@ -45,15 +49,21 @@ def tile_terowparallellinear_kernel(tc, input_, weight, bias, grad_out, out):
         g_codes = keep.tile([P, OUT], U32, name="g_codes", align_bytes=64)
         g_scales = keep.tile([P, OUT], U8, name="g_scales", align_bytes=64)
 
-        nc.sync.dma_start(out=xh_raw[:], in_=x[:, 0:HEAD].rearrange("(p j) w -> p j w", j=PACK))
         nc.sync.dma_start(out=g_raw[:], in_=g.rearrange("(p j) w -> p j w", j=PACK))
-        nc.sync.dma_start(out=xr_raw[:], in_=x[:, HEAD:IN].rearrange("(p j) w -> p j w", j=PACK))
+        for i in range(3):
+            nc.sync.dma_start(
+                out=x_raw[i][:],
+                in_=x[:, LOADS[i] : LOADS[i + 1]].rearrange("(p j) w -> p j w", j=PACK),
+            )
 
         def regroup(copy, grp, raw, base, lo, hi):
             copy(
                 out=grp[:, lo:hi, :].rearrange("p (c i) t -> p c t i", i=4),
                 in_=raw[:, :, lo - base : hi - base].rearrange("p t (c i) -> p c t i", i=4),
             )
+
+        def regroup_x(copy, i, lo, hi):
+            regroup(copy, x_grp, x_raw[i], LOADS[i], lo, hi)
 
         def quantise(grp, codes, scales, fmt, lo, hi):
             nc.vector.quantize_mx(
@@ -68,51 +78,54 @@ def tile_terowparallellinear_kernel(tc, input_, weight, bias, grad_out, out):
         def quantise_g(lo, hi):
             quantise(g_grp, g_codes, g_scales, E5M2X4, lo, hi)
 
-        def product(b, n, copy, dest):
-            acc = psum.tile([P, N_TILE], F32, name="acc")
-            nc.tensor.matmul_mx(
-                out=acc[:],
-                lhsT=g_codes[:, b * P : (b + 1) * P].bitcast(E5M2X4),
-                lhsT_scale=g_scales[:, b * P : (b + 1) * P],
-                rhs=x_codes[:, n * N_TILE : (n + 1) * N_TILE].bitcast(E4M3X4),
-                rhs_scale=x_scales[:, n * N_TILE : (n + 1) * N_TILE],
-                start=True,
-                stop=True,
-            )
-            copy(out=dest, in_=acc[:])
-
         vcopy = nc.vector.tensor_copy
         scopy = nc.scalar.copy
 
-        regroup(vcopy, x_grp, xh_raw, 0, 0, 768)
-        regroup(scopy, x_grp, xh_raw, 0, 768, 1536)
-        quantise_x(0, 512)
+        def strip(pool, b, n_lo, n_hi, engines):
+            res = pool.tile([P, (n_hi - n_lo) * N_TILE], F32, name="res")
+            for n in range(n_lo, n_hi):
+                acc = psum.tile([P, N_TILE], F32, name="acc")
+                nc.tensor.matmul_mx(
+                    out=acc[:],
+                    lhsT=g_codes[:, b * P : (b + 1) * P].bitcast(E5M2X4),
+                    lhsT_scale=g_scales[:, b * P : (b + 1) * P],
+                    rhs=x_codes[:, n * N_TILE : (n + 1) * N_TILE].bitcast(E4M3X4),
+                    rhs_scale=x_scales[:, n * N_TILE : (n + 1) * N_TILE],
+                    start=True,
+                    stop=True,
+                )
+                engines[n - n_lo](
+                    out=res[:, (n - n_lo) * N_TILE : (n - n_lo + 1) * N_TILE], in_=acc[:]
+                )
+            nc.sync.dma_start(
+                out=out[b * P : (b + 1) * P, n_lo * N_TILE : n_hi * N_TILE], in_=res[:]
+            )
+
+        def alternate(b, count):
+            return [scopy if (k + b) % 2 == 0 else vcopy for k in range(count)]
+
         regroup(vcopy, g_grp, g_raw, 0, 0, 512)
         regroup(scopy, g_grp, g_raw, 0, 512, 1024)
-        quantise_x(512, 1024)
         quantise_g(0, 512)
-        quantise_x(1024, 1536)
+        regroup_x(vcopy, 0, 0, 512)
+        regroup_x(scopy, 0, 512, 1024)
+        quantise_x(0, 512)
         quantise_g(512, 1024)
+        quantise_x(512, 1024)
 
-        head_tiles = HEAD // N_TILE
         for b in range(BLOCKS):
-            res = stage_a.tile([P, HEAD], F32, name="res_a")
-            for n in range(head_tiles):
-                copy = vcopy if (b < 3 and n == head_tiles - 1) else scopy
-                product(b, n, copy, res[:, n * N_TILE : (n + 1) * N_TILE])
-            nc.sync.dma_start(out=out[b * P : (b + 1) * P, 0:HEAD], in_=res[:])
-            if b == 2:
-                regroup(vcopy, x_grp, xr_raw, HEAD, 1536, 2560)
-                regroup(vcopy, x_grp, xr_raw, HEAD, 2560, 3584)
-                quantise_x(1536, 2560)
-                regroup(vcopy, x_grp, xr_raw, HEAD, 3584, 4096)
-                quantise_x(2560, 3584)
-                quantise_x(3584, 4096)
+            strip(stage2, b, 0, 2, [scopy, vcopy if b < EARLY_V else scopy])
 
-        rest_tiles = REST // N_TILE
-        for b in range(BLOCKS):
-            res = stage_b.tile([P, REST], F32, name="res_b")
-            for n in range(rest_tiles):
-                copy = scopy if (n + b) % 2 == 0 else vcopy
-                product(b, head_tiles + n, copy, res[:, n * N_TILE : (n + 1) * N_TILE])
-            nc.sync.dma_start(out=out[b * P : (b + 1) * P, HEAD:IN], in_=res[:])
+        regroup_x(vcopy, 1, 1024, 2048)
+        regroup_x(vcopy, 2, 2048, 3072)
+        quantise_x(1024, 2048)
+        regroup_x(vcopy, 2, 3072, 4096)
+        quantise_x(2048, 3072)
+        quantise_x(3072, 4096)
+
+        for b in range(SPLIT_ROWS):
+            strip(stage2, b, 2, 4, [scopy, scopy])
+        for b in range(SPLIT_ROWS):
+            strip(stage4, b, 4, 8, alternate(b, 4))
+        for b in range(SPLIT_ROWS, BLOCKS):
+            strip(stage6, b, 2, 8, alternate(b, 6))

@@ -17,8 +17,8 @@ OUT = 1024
 N_TILE = 512
 BLOCKS = OUT // P
 LOADS = (0, 1024, 2048, 4096)
-SPLIT_ROWS = 4
-EARLY_V = 3
+SPLIT_ROWS = 6
+EARLY_V = 5
 
 FLOPS = 2 * TOKENS * IN * OUT
 BYTES = TOKENS * IN * 2 + TOKENS * OUT * 2 + OUT * IN * 4
@@ -31,9 +31,9 @@ def tile_terowparallellinear_kernel(tc, input_, weight, bias, grad_out, out):
 
     with ExitStack() as ctx:
         keep = ctx.enter_context(tc.tile_pool(name="keep", bufs=1))
-        stage2 = ctx.enter_context(tc.tile_pool(name="stage2", bufs=8))
-        stage4 = ctx.enter_context(tc.tile_pool(name="stage4", bufs=4))
-        stage6 = ctx.enter_context(tc.tile_pool(name="stage6", bufs=3))
+        stage2 = ctx.enter_context(tc.tile_pool(name="stage2", bufs=10))
+        stage4 = ctx.enter_context(tc.tile_pool(name="stage4", bufs=6))
+        stage6 = ctx.enter_context(tc.tile_pool(name="stage6", bufs=2))
         psum = ctx.enter_context(tc.psum_pool(name="psum", bufs=8))
         ctx.enter_context(tc.manual_schedule())
 
@@ -104,11 +104,22 @@ def tile_terowparallellinear_kernel(tc, input_, weight, bias, grad_out, out):
         def alternate(b, count):
             return [scopy if (k + b) % 2 == 0 else vcopy for k in range(count)]
 
+        def warm(src, count):
+            for k in range(count):
+                idle = psum.tile([P, N_TILE], F32, name="acc")
+                nc.tensor.matmul(
+                    out=idle[:], lhsT=src[:, 0:P], rhs=src[:, 0:N_TILE], start=True, stop=True
+                )
+
+        warm(g_raw[:, 0, :], 4)
+        warm(x_raw[0][:, 0, :], 4)
+
         regroup(vcopy, g_grp, g_raw, 0, 0, 512)
         regroup(scopy, g_grp, g_raw, 0, 512, 1024)
         quantise_g(0, 512)
         regroup_x(vcopy, 0, 0, 512)
         regroup_x(scopy, 0, 512, 1024)
+        warm(x_grp[:, 0:512, :].rearrange("p w j -> p (w j)"), 2)
         quantise_x(0, 512)
         quantise_g(512, 1024)
         quantise_x(512, 1024)
@@ -116,11 +127,14 @@ def tile_terowparallellinear_kernel(tc, input_, weight, bias, grad_out, out):
         for b in range(BLOCKS):
             strip(stage2, b, 0, 2, [scopy, vcopy if b < EARLY_V else scopy])
 
-        regroup_x(vcopy, 1, 1024, 2048)
+        regroup_x(vcopy, 1, 1024, 1536)
+        regroup_x(vcopy, 1, 1536, 2048)
+        quantise_x(1024, 1536)
+        quantise_x(1536, 2048)
         regroup_x(vcopy, 2, 2048, 3072)
-        quantise_x(1024, 2048)
-        regroup_x(vcopy, 2, 3072, 4096)
+        regroup_x(vcopy, 2, 3072, 3584)
         quantise_x(2048, 3072)
+        regroup_x(vcopy, 2, 3584, 4096)
         quantise_x(3072, 4096)
 
         for b in range(SPLIT_ROWS):

@@ -16,7 +16,7 @@ IN = 4096
 OUT = 1024
 N_TILE = 512
 BLOCKS = OUT // P
-LOADS = (0, 1024, 2048, 4096)
+LOADS = (0, 1024, 4096)
 SPLIT_ROWS = 6
 EARLY_V = 5
 
@@ -40,7 +40,7 @@ def tile_terowparallellinear_kernel(tc, input_, weight, bias, grad_out, out):
         g_raw = keep.tile([P, PACK, OUT], BF16, name="g_raw")
         x_raw = [
             keep.tile([P, PACK, LOADS[i + 1] - LOADS[i]], BF16, name="x_raw%d" % i)
-            for i in range(3)
+            for i in range(2)
         ]
         x_grp = keep.tile([P, IN, PACK], BF16, name="x_grp", align_bytes=64)
         g_grp = keep.tile([P, OUT, PACK], BF16, name="g_grp", align_bytes=64)
@@ -50,7 +50,7 @@ def tile_terowparallellinear_kernel(tc, input_, weight, bias, grad_out, out):
         g_scales = keep.tile([P, OUT], U8, name="g_scales", align_bytes=64)
 
         nc.sync.dma_start(out=g_raw[:], in_=g.rearrange("(p j) w -> p j w", j=PACK))
-        for i in range(3):
+        for i in range(2):
             nc.sync.dma_start(
                 out=x_raw[i][:],
                 in_=x[:, LOADS[i] : LOADS[i + 1]].rearrange("(p j) w -> p j w", j=PACK),
@@ -131,10 +131,10 @@ def tile_terowparallellinear_kernel(tc, input_, weight, bias, grad_out, out):
         regroup_x(vcopy, 1, 1536, 2048)
         quantise_x(1024, 1536)
         quantise_x(1536, 2048)
-        regroup_x(vcopy, 2, 2048, 3072)
-        regroup_x(vcopy, 2, 3072, 3584)
+        regroup_x(vcopy, 1, 2048, 3072)
+        regroup_x(vcopy, 1, 3072, 3584)
         quantise_x(2048, 3072)
-        regroup_x(vcopy, 2, 3584, 4096)
+        regroup_x(vcopy, 1, 3584, 4096)
         quantise_x(3072, 4096)
 
         for b in range(SPLIT_ROWS):

@@ -114,17 +114,19 @@ def tile_terowparallellinear_kernel(tc, input_, weight, bias, grad_out, out):
         warm(g_raw[:, 0, :], 4)
         warm(x_raw[0][:, 0, :], 4)
 
-        regroup(vcopy, g_grp, g_raw, 0, 0, 512)
-        regroup(scopy, g_grp, g_raw, 0, 512, 1024)
+        regroup(vcopy, g_grp, g_raw, 0, 0, 640)
+        regroup(scopy, g_grp, g_raw, 0, 640, 1024)
         quantise_g(0, 512)
         regroup_x(vcopy, 0, 0, 512)
-        regroup_x(scopy, 0, 512, 1024)
+        regroup_x(scopy, 0, 704, 1024)
+        regroup_x(vcopy, 0, 512, 704)
         warm(x_grp[:, 0:512, :].rearrange("p w j -> p (w j)"), 2)
         quantise_x(0, 512)
-        quantise_g(512, 1024)
         quantise_x(512, 1024)
 
         for b in range(BLOCKS):
+            if b == 2:
+                quantise_g(512, 1024)
             strip(stage2, b, 0, 2, [scopy, vcopy if b < EARLY_V else scopy])
 
         regroup_x(vcopy, 1, 1024, 1536)

@@ -19,6 +19,7 @@ BLOCKS = OUT // P
 LOADS = (0, 1024, 4096)
 SPLIT_ROWS = 6
 EARLY_V = 5
+SINGLE_ROWS = 3
 
 FLOPS = 2 * TOKENS * IN * OUT
 BYTES = TOKENS * IN * 2 + TOKENS * OUT * 2 + OUT * IN * 4
@@ -31,7 +32,8 @@ def tile_terowparallellinear_kernel(tc, input_, weight, bias, grad_out, out):
 
     with ExitStack() as ctx:
         keep = ctx.enter_context(tc.tile_pool(name="keep", bufs=1))
-        stage2 = ctx.enter_context(tc.tile_pool(name="stage2", bufs=10))
+        stage1 = ctx.enter_context(tc.tile_pool(name="stage1", bufs=6))
+        stage2 = ctx.enter_context(tc.tile_pool(name="stage2", bufs=8))
         stage4 = ctx.enter_context(tc.tile_pool(name="stage4", bufs=6))
         stage6 = ctx.enter_context(tc.tile_pool(name="stage6", bufs=2))
         psum = ctx.enter_context(tc.psum_pool(name="psum", bufs=8))
@@ -117,15 +119,20 @@ def tile_terowparallellinear_kernel(tc, input_, weight, bias, grad_out, out):
         regroup(vcopy, g_grp, g_raw, 0, 0, 640)
         regroup(scopy, g_grp, g_raw, 0, 640, 1024)
         quantise_g(0, 512)
-        regroup_x(vcopy, 0, 0, 512)
-        regroup_x(scopy, 0, 704, 1024)
-        regroup_x(vcopy, 0, 512, 704)
+        regroup_x(vcopy, 0, 0, 352)
+        regroup_x(scopy, 0, 352, 512)
+        regroup_x(scopy, 0, 864, 1024)
         warm(x_grp[:, 0:512, :].rearrange("p w j -> p (w j)"), 2)
         quantise_x(0, 512)
+        regroup_x(vcopy, 0, 512, 864)
         quantise_x(512, 1024)
 
-        for b in range(BLOCKS):
-            if b == 2:
+        for b in range(SINGLE_ROWS):
+            strip(stage1, b, 0, 1, [scopy])
+        for b in range(SINGLE_ROWS):
+            strip(stage1, b, 1, 2, [vcopy])
+        for b in range(SINGLE_ROWS, BLOCKS):
+            if b == SINGLE_ROWS:
                 quantise_g(512, 1024)
             strip(stage2, b, 0, 2, [scopy, vcopy if b < EARLY_V else scopy])
 

@@ -19,7 +19,6 @@ BLOCKS = OUT // P
 LOADS = (0, 1024, 4096)
 SPLIT_ROWS = 6
 EARLY_V = 5
-SINGLE_ROWS = 3
 
 FLOPS = 2 * TOKENS * IN * OUT
 BYTES = TOKENS * IN * 2 + TOKENS * OUT * 2 + OUT * IN * 4
@@ -32,8 +31,9 @@ def tile_terowparallellinear_kernel(tc, input_, weight, bias, grad_out, out):
 
     with ExitStack() as ctx:
         keep = ctx.enter_context(tc.tile_pool(name="keep", bufs=1))
-        stage1 = ctx.enter_context(tc.tile_pool(name="stage1", bufs=6))
-        stage2 = ctx.enter_context(tc.tile_pool(name="stage2", bufs=8))
+        stage1 = ctx.enter_context(tc.tile_pool(name="stage1", bufs=1))
+        stage2 = ctx.enter_context(tc.tile_pool(name="stage2", bufs=10))
+        stage3 = ctx.enter_context(tc.tile_pool(name="stage3", bufs=1))
         stage4 = ctx.enter_context(tc.tile_pool(name="stage4", bufs=6))
         stage6 = ctx.enter_context(tc.tile_pool(name="stage6", bufs=2))
         psum = ctx.enter_context(tc.psum_pool(name="psum", bufs=8))
@@ -119,22 +119,20 @@ def tile_terowparallellinear_kernel(tc, input_, weight, bias, grad_out, out):
         regroup(vcopy, g_grp, g_raw, 0, 0, 640)
         regroup(scopy, g_grp, g_raw, 0, 640, 1024)
         quantise_g(0, 512)
-        regroup_x(vcopy, 0, 0, 352)
-        regroup_x(scopy, 0, 352, 512)
-        regroup_x(scopy, 0, 864, 1024)
+        regroup_x(vcopy, 0, 0, 512)
+        regroup_x(scopy, 0, 704, 1024)
+        regroup_x(vcopy, 0, 512, 704)
         warm(x_grp[:, 0:512, :].rearrange("p w j -> p (w j)"), 2)
         quantise_x(0, 512)
-        regroup_x(vcopy, 0, 512, 864)
         quantise_x(512, 1024)
 
-        for b in range(SINGLE_ROWS):
-            strip(stage1, b, 0, 1, [scopy])
-        for b in range(SINGLE_ROWS):
-            strip(stage1, b, 1, 2, [vcopy])
-        for b in range(SINGLE_ROWS, BLOCKS):
-            if b == SINGLE_ROWS:
+        for b in range(BLOCKS):
+            if b == 2:
                 quantise_g(512, 1024)
-            strip(stage2, b, 0, 2, [scopy, vcopy if b < EARLY_V else scopy])
+            if b == 0:
+                strip(stage1, b, 0, 1, [scopy])
+            else:
+                strip(stage2, b, 0, 2, [scopy, vcopy if b < EARLY_V else scopy])
 
         regroup_x(vcopy, 1, 1024, 1536)
         regroup_x(vcopy, 1, 1536, 2048)
@@ -146,7 +144,8 @@ def tile_terowparallellinear_kernel(tc, input_, weight, bias, grad_out, out):
         regroup_x(vcopy, 1, 3584, 4096)
         quantise_x(3072, 4096)
 
-        for b in range(SPLIT_ROWS):
+        strip(stage3, 0, 1, 4, [scopy, scopy, scopy])
+        for b in range(1, SPLIT_ROWS):
             strip(stage2, b, 2, 4, [scopy, scopy])
         for b in range(SPLIT_ROWS):
             strip(stage4, b, 4, 8, alternate(b, 4))

from contextlib import ExitStack

import concourse.mybir as mybir

BF16 = mybir.dt.bfloat16
F32 = mybir.dt.float32
U32 = mybir.dt.uint32
U8 = mybir.dt.uint8
E4M3X4 = mybir.dt.float8_e4m3fn_x4
E5M2X4 = mybir.dt.float8_e5m2_x4

P = 128
PACK = 4
TOKENS = 512
IN = 4096
OUT = 1024
N_TILE = 512
BLOCKS = OUT // P
LOADS = (0, 1024, 4096)
SPLIT_ROWS = 6
EARLY_V = 5

FLOPS = 2 * TOKENS * IN * OUT
BYTES = TOKENS * IN * 2 + TOKENS * OUT * 2 + OUT * IN * 4


def tile_terowparallellinear_kernel(tc, input_, weight, bias, grad_out, out):
    nc = tc.nc
    x = input_.flatten_outer_dims()
    g = grad_out.flatten_outer_dims()

    with ExitStack() as ctx:
        keep = ctx.enter_context(tc.tile_pool(name="keep", bufs=1))
        stage1 = ctx.enter_context(tc.tile_pool(name="stage1", bufs=1))
        stage2 = ctx.enter_context(tc.tile_pool(name="stage2", bufs=10))
        stage3 = ctx.enter_context(tc.tile_pool(name="stage3", bufs=1))
        stage4 = ctx.enter_context(tc.tile_pool(name="stage4", bufs=6))
        stage6 = ctx.enter_context(tc.tile_pool(name="stage6", bufs=2))
        psum = ctx.enter_context(tc.psum_pool(name="psum", bufs=8))
        ctx.enter_context(tc.manual_schedule())

        g_raw = keep.tile([P, PACK, OUT], BF16, name="g_raw")
        x_raw = [
            keep.tile([P, PACK, LOADS[i + 1] - LOADS[i]], BF16, name="x_raw%d" % i)
            for i in range(2)
        ]
        x_grp = keep.tile([P, IN, PACK], BF16, name="x_grp", align_bytes=64)
        g_grp = keep.tile([P, OUT, PACK], BF16, name="g_grp", align_bytes=64)
        x_codes = keep.tile([P, IN], U32, name="x_codes", align_bytes=64)
        x_scales = keep.tile([P, IN], U8, name="x_scales", align_bytes=64)
        g_codes = keep.tile([P, OUT], U32, name="g_codes", align_bytes=64)
        g_scales = keep.tile([P, OUT], U8, name="g_scales", align_bytes=64)

        nc.sync.dma_start(out=g_raw[:], in_=g.rearrange("(p j) w -> p j w", j=PACK))
        for i in range(2):
            nc.sync.dma_start(
                out=x_raw[i][:],
                in_=x[:, LOADS[i] : LOADS[i + 1]].rearrange("(p j) w -> p j w", j=PACK),
            )

        def regroup(copy, grp, raw, base, lo, hi):
            copy(
                out=grp[:, lo:hi, :].rearrange("p (c i) t -> p c t i", i=4),
                in_=raw[:, :, lo - base : hi - base].rearrange("p t (c i) -> p c t i", i=4),
            )

        def regroup_x(copy, i, lo, hi):
            regroup(copy, x_grp, x_raw[i], LOADS[i], lo, hi)

        def quantise(grp, codes, scales, fmt, lo, hi):
            nc.vector.quantize_mx(
                out=codes[:, lo:hi].bitcast(fmt),
                scales=scales[:, lo:hi],
                in_=grp[:, lo:hi, :].rearrange("p w j -> p (w j)"),
            )

        def quantise_x(lo, hi):
            quantise(x_grp, x_codes, x_scales, E4M3X4, lo, hi)

        def quantise_g(lo, hi):
            quantise(g_grp, g_codes, g_scales, E5M2X4, lo, hi)

        vcopy = nc.vector.tensor_copy
        scopy = nc.scalar.copy

        def strip(pool, b, n_lo, n_hi, engines):
            res = pool.tile([P, (n_hi - n_lo) * N_TILE], F32, name="res")
            for n in range(n_lo, n_hi):
                acc = psum.tile([P, N_TILE], F32, name="acc")
                nc.tensor.matmul_mx(
                    out=acc[:],
                    lhsT=g_codes[:, b * P : (b + 1) * P].bitcast(E5M2X4),
                    lhsT_scale=g_scales[:, b * P : (b + 1) * P],
                    rhs=x_codes[:, n * N_TILE : (n + 1) * N_TILE].bitcast(E4M3X4),
                    rhs_scale=x_scales[:, n * N_TILE : (n + 1) * N_TILE],
                    start=True,
                    stop=True,
                )
                engines[n - n_lo](
                    out=res[:, (n - n_lo) * N_TILE : (n - n_lo + 1) * N_TILE], in_=acc[:]
                )
            nc.sync.dma_start(
                out=out[b * P : (b + 1) * P, n_lo * N_TILE : n_hi * N_TILE], in_=res[:]
            )

        def alternate(b, count):
            return [scopy if (k + b) % 2 == 0 else vcopy for k in range(count)]

        def warm(src, count):
            for k in range(count):
                idle = psum.tile([P, N_TILE], F32, name="acc")
                nc.tensor.matmul(
                    out=idle[:], lhsT=src[:, 0:P], rhs=src[:, 0:N_TILE], start=True, stop=True
                )

        warm(g_raw[:, 0, :], 4)
        warm(x_raw[0][:, 0, :], 4)

        regroup(vcopy, g_grp, g_raw, 0, 0, 640)
        regroup(scopy, g_grp, g_raw, 0, 640, 1024)
        quantise_g(0, 512)
        regroup_x(vcopy, 0, 0, 512)
        regroup_x(scopy, 0, 704, 1024)
        regroup_x(vcopy, 0, 512, 704)
        warm(x_grp[:, 0:512, :].rearrange("p w j -> p (w j)"), 2)
        quantise_x(0, 512)
        quantise_x(512, 1024)

        for b in range(BLOCKS):
            if b == 2:
                quantise_g(512, 1024)
            if b == 0:
                strip(stage1, b, 0, 1, [scopy])
            else:
                strip(stage2, b, 0, 2, [scopy, vcopy if b < EARLY_V else scopy])

        regroup_x(vcopy, 1, 1024, 1536)
        regroup_x(vcopy, 1, 1536, 2048)
        quantise_x(1024, 1536)
        quantise_x(1536, 2048)
        regroup_x(vcopy, 1, 2048, 3072)
        regroup_x(vcopy, 1, 3072, 3584)
        quantise_x(2048, 3072)
        regroup_x(vcopy, 1, 3584, 4096)
        quantise_x(3072, 4096)

        strip(stage3, 0, 1, 4, [scopy, scopy, scopy])
        for b in range(1, SPLIT_ROWS):
            strip(stage2, b, 2, 4, [scopy, scopy])
        for b in range(SPLIT_ROWS):
            strip(stage4, b, 4, 8, alternate(b, 4))
        for b in range(SPLIT_ROWS, BLOCKS):
            strip(stage6, b, 2, 8, alternate(b, 6))
